import numpy as np
import ml_dtypes

BF16 = ml_dtypes.bfloat16


def bf(x):
    return np.asarray(x, np.float32).astype(BF16)


def f32(x):
    return np.asarray(x, np.float32)


def f64(x):
    return np.asarray(x).astype(np.float64)


def striped(idx):
    return np.tile(idx.reshape(-1, 16).T, (8, 1))


H, KX, M, S, N = 128, 640, 512, 256, 128


def sigmoid(v):
    return 1.0 / (1.0 + np.exp(-v))


def setup_inputs():
    return {
        "base": f32(0.3 * np.random.standard_normal((H, S))),
        "x": bf(np.random.standard_normal((KX, N))),
        "h_prev": bf(0.3 * np.random.standard_normal((H, N))),
        "c_prev": f32(0.5 * np.random.standard_normal((H, N))),
        "wx": bf(np.random.standard_normal((KX, M)) / np.sqrt(KX)),
        "wh": bf(np.random.standard_normal((H, M)) / np.sqrt(H)),
        "b": f32(0.1 * np.random.standard_normal((M, 1))),
        "offs": striped(np.random.permutation(S)[:N]),
    }


def reference(base, x, h_prev, c_prev, wx, wh, b, offs):
    idx = offs[:16].T.reshape(-1)
    z = f64(wx).T @ f64(x) + f64(wh).T @ f64(h_prev) + f64(b)
    zi, zf, zu, zo = z.reshape(-1, H, N)
    c_new = sigmoid(zf) * f64(c_prev) + sigmoid(zi) * np.tanh(zu)
    out = f64(base).copy()
    out[:, idx] = sigmoid(zo) * np.tanh(c_new)
    return out

@@ -1,0 +1,76 @@
+import concourse.mybir as mybir
+
+BF16, F32, U16 = mybir.dt.bfloat16, mybir.dt.float32, mybir.dt.uint16
+SIGMOID = mybir.ActivationFunctionType.Sigmoid
+TANH = mybir.ActivationFunctionType.Tanh
+MULT, ADD = mybir.AluOpType.mult, mybir.AluOpType.add
+
+P = 128
+KX, M, S, N = 640, 512, 256, 128
+KB = KX // P
+GATE_I, GATE_F, GATE_U, GATE_O = 0, 1, 2, 3
+
+FLOPS = 2 * (KX + P) * M * N
+
+
+def tile_deepmultipledecoder_kernel(tc, base, x, h_prev, c_prev, wx, wh, b, offs, out):
+    nc = tc.nc
+    with (
+        tc.tile_pool(name="held", bufs=1) as held,
+        tc.psum_pool(name="psum", bufs=1) as psum,
+    ):
+        offsets = held.tile([P, N // 16], U16, name="offsets")
+        nc.sync.dma_start(offsets[:], offs)
+
+        h_sb = held.tile([P, N], BF16, name="h_sb")
+        nc.scalar.dma_start(h_sb[:], h_prev)
+        wh_sb = held.tile([P, M], BF16, name="wh_sb")
+        nc.scalar.dma_start(wh_sb[:], wh)
+        x_sb = held.tile([P, KB, N], BF16, name="x_sb")
+        nc.sync.dma_start(x_sb[:], x.rearrange("(kb p) n -> p kb n", p=P))
+        wx_sb = [held.tile([P, M], BF16, name=f"wx_sb{kb}") for kb in range(KB)]
+        for kb in range(KB):
+            queue = nc.sync if kb % 2 == 0 else nc.scalar
+            queue.dma_start(wx_sb[kb][:], wx[kb * P : (kb + 1) * P, :])
+
+        b_sb = held.tile([P, 4], F32, name="b_sb")
+        with nc.allow_non_contiguous_dma(reason="512 bias values, one to a partition and gate"):
+            nc.gpsimd.dma_start(b_sb[:], b.rearrange("(g p) o -> p (g o)", p=P))
+        c_sb = held.tile([P, N], F32, name="c_sb")
+        nc.sync.dma_start(c_sb[:], c_prev)
+        window = held.tile([P, S], F32, name="window")
+        nc.scalar.dma_start(window[:], base)
+
+        z = [psum.tile([P, N], F32, name=f"z{g}") for g in range(4)]
+        blocks = [(wh_sb, h_sb[:])] + [(wx_sb[kb], x_sb[:, kb, :]) for kb in range(KB)]
+        for k, (weights, moving) in enumerate(blocks):
+            for g in (GATE_F, GATE_I, GATE_U, GATE_O):
+                nc.tensor.matmul(
+                    z[g][:],
+                    weights[:, g * P : (g + 1) * P],
+                    moving,
+                    start=(k == 0),
+                    stop=(k == len(blocks) - 1),
+                )
+
+        def gate(g, func, name):
+            result = held.tile([P, N], F32, name=name)
+            nc.scalar.activation(result[:], z[g][:], func, bias=b_sb[:, g : g + 1])
+            return result
+
+        sig_f = gate(GATE_F, SIGMOID, "sig_f")
+        sig_i = gate(GATE_I, SIGMOID, "sig_i")
+        tanh_u = gate(GATE_U, TANH, "tanh_u")
+        sig_o = gate(GATE_O, SIGMOID, "sig_o")
+
+        kept = held.tile([P, N], F32, name="kept")
+        nc.vector.tensor_tensor(kept[:], sig_f[:], c_sb[:], MULT)
+        fresh = held.tile([P, N], F32, name="fresh")
+        nc.vector.tensor_tensor(fresh[:], sig_i[:], tanh_u[:], MULT)
+        c_new = held.tile([P, N], F32, name="c_new")
+        nc.vector.tensor_tensor(c_new[:], kept[:], fresh[:], ADD)
+        tanh_c = held.tile([P, N], F32, name="tanh_c")
+        nc.scalar.activation(tanh_c[:], c_new[:], TANH)
+
+        nc.vector.tensor_tensor(window[:].indirect(offsets[:]), sig_o[:], tanh_c[:], MULT)
+        nc.sync.dma_start(out, window[:])

@@ -22,6 +22,10 @@ def tile_deepmultipledecoder_kernel(tc, base, x, h_prev, c_prev, wx, wh, b, offs
         offsets = held.tile([P, N // 16], U16, name="offsets")
         nc.sync.dma_start(offsets[:], offs)
 
+        b_sb = held.tile([P, 4], F32, name="b_sb")
+        with nc.allow_non_contiguous_dma(reason="512 bias values, one to a partition and gate"):
+            nc.sync.dma_start(b_sb[:], b.rearrange("(g p) o -> p (g o)", p=P))
+
         h_sb = held.tile([P, N], BF16, name="h_sb")
         nc.scalar.dma_start(h_sb[:], h_prev)
         wh_sb = held.tile([P, M], BF16, name="wh_sb")
@@ -33,13 +37,15 @@ def tile_deepmultipledecoder_kernel(tc, base, x, h_prev, c_prev, wx, wh, b, offs
             queue = nc.sync if kb % 2 == 0 else nc.scalar
             queue.dma_start(wx_sb[kb][:], wx[kb * P : (kb + 1) * P, :])
 
-        b_sb = held.tile([P, 4], F32, name="b_sb")
-        with nc.allow_non_contiguous_dma(reason="512 bias values, one to a partition and gate"):
-            nc.gpsimd.dma_start(b_sb[:], b.rearrange("(g p) o -> p (g o)", p=P))
         c_sb = held.tile([P, N], F32, name="c_sb")
         nc.sync.dma_start(c_sb[:], c_prev)
         window = held.tile([P, S], F32, name="window")
         nc.scalar.dma_start(window[:], base)
+
+        zeros = held.tile([P, 1], F32, name="zeros")
+        nc.vector.memset(zeros[:], 0.0)
+        early = held.tile([P, 1], F32, name="early")
+        nc.scalar.activation(early[:], zeros[:, 0:1], SIGMOID)
 
         z = [psum.tile([P, N], F32, name=f"z{g}") for g in range(4)]
         blocks = [(wh_sb, h_sb[:])] + [(wx_sb[kb], x_sb[:, kb, :]) for kb in range(KB)]

@@ -10,6 +10,8 @@ KX, M, S, N = 640, 512, 256, 128
 KB = KX // P
 GATE_I, GATE_F, GATE_U, GATE_O = 0, 1, 2, 3
 
+WARM_UP = 4
+
 FLOPS = 2 * (KX + P) * M * N
 
 
@@ -42,10 +44,13 @@ def tile_deepmultipledecoder_kernel(tc, base, x, h_prev, c_prev, wx, wh, b, offs
         window = held.tile([P, S], F32, name="window")
         nc.scalar.dma_start(window[:], base)
 
-        zeros = held.tile([P, 1], F32, name="zeros")
+        zeros = held.tile([P, 512], BF16, name="zeros")
         nc.vector.memset(zeros[:], 0.0)
         early = held.tile([P, 1], F32, name="early")
         nc.scalar.activation(early[:], zeros[:, 0:1], SIGMOID)
+        idle_bank = psum.tile([P, 512], F32, name="idle_bank")
+        for i in range(WARM_UP):
+            nc.tensor.matmul(idle_bank[:], zeros[:, 0:P], zeros[:], start=True, stop=True)
 
         z = [psum.tile([P, N], F32, name=f"z{g}") for g in range(4)]
         blocks = [(wh_sb, h_sb[:])] + [(wx_sb[kb], x_sb[:, kb, :]) for kb in range(KB)]

@@ -33,16 +33,17 @@ def tile_deepmultipledecoder_kernel(tc, base, x, h_prev, c_prev, wx, wh, b, offs
         wh_sb = held.tile([P, M], BF16, name="wh_sb")
         nc.scalar.dma_start(wh_sb[:], wh)
         x_sb = held.tile([P, KB, N], BF16, name="x_sb")
-        nc.sync.dma_start(x_sb[:], x.rearrange("(kb p) n -> p kb n", p=P))
+        nc.sync.dma_start(x_sb[:], x.rearrange("(p kb) n -> p kb n", kb=KB))
+        wx_blocks = wx.rearrange("(p kb) m -> kb p m", kb=KB)
         wx_sb = [held.tile([P, M], BF16, name=f"wx_sb{kb}") for kb in range(KB)]
         for kb in range(KB):
             queue = nc.sync if kb % 2 == 0 else nc.scalar
-            queue.dma_start(wx_sb[kb][:], wx[kb * P : (kb + 1) * P, :])
+            queue.dma_start(wx_sb[kb][:], wx_blocks[kb])
 
         c_sb = held.tile([P, N], F32, name="c_sb")
         nc.sync.dma_start(c_sb[:], c_prev)
         window = held.tile([P, S], F32, name="window")
-        nc.scalar.dma_start(window[:], base)
+        nc.sync.dma_start(window[:], base)
 
         zeros = held.tile([P, 512], BF16, name="zeros")
         nc.vector.memset(zeros[:], 0.0)
@@ -54,15 +55,22 @@ def tile_deepmultipledecoder_kernel(tc, base, x, h_prev, c_prev, wx, wh, b, offs
 
         z = [psum.tile([P, N], F32, name=f"z{g}") for g in range(4)]
         blocks = [(wh_sb, h_sb[:])] + [(wx_sb[kb], x_sb[:, kb, :]) for kb in range(KB)]
-        for k, (weights, moving) in enumerate(blocks):
-            for g in (GATE_F, GATE_I, GATE_U, GATE_O):
-                nc.tensor.matmul(
-                    z[g][:],
-                    weights[:, g * P : (g + 1) * P],
-                    moving,
-                    start=(k == 0),
-                    stop=(k == len(blocks) - 1),
-                )
+
+        def add_block(g, k):
+            weights, moving = blocks[k]
+            nc.tensor.matmul(
+                z[g][:],
+                weights[:, g * P : (g + 1) * P],
+                moving,
+                start=(k == 0),
+                stop=(k == len(blocks) - 1),
+            )
+
+        for k in range(len(blocks)):
+            for g in (GATE_F, GATE_I, GATE_U):
+                add_block(g, k)
+        for k in range(len(blocks)):
+            add_block(GATE_O, k)
 
         def gate(g, func, name):
             result = held.tile([P, N], F32, name=name)

@@ -55,22 +55,15 @@ def tile_deepmultipledecoder_kernel(tc, base, x, h_prev, c_prev, wx, wh, b, offs
 
         z = [psum.tile([P, N], F32, name=f"z{g}") for g in range(4)]
         blocks = [(wh_sb, h_sb[:])] + [(wx_sb[kb], x_sb[:, kb, :]) for kb in range(KB)]
-
-        def add_block(g, k):
-            weights, moving = blocks[k]
-            nc.tensor.matmul(
-                z[g][:],
-                weights[:, g * P : (g + 1) * P],
-                moving,
-                start=(k == 0),
-                stop=(k == len(blocks) - 1),
-            )
-
-        for k in range(len(blocks)):
-            for g in (GATE_F, GATE_I, GATE_U):
-                add_block(g, k)
-        for k in range(len(blocks)):
-            add_block(GATE_O, k)
+        for k, (weights, moving) in enumerate(blocks):
+            for g in (GATE_F, GATE_I, GATE_U, GATE_O):
+                nc.tensor.matmul(
+                    z[g][:],
+                    weights[:, g * P : (g + 1) * P],
+                    moving,
+                    start=(k == 0),
+                    stop=(k == len(blocks) - 1),
+                )
 
         def gate(g, func, name):
             result = held.tile([P, N], F32, name=name)

@@ -9,7 +9,7 @@ P = 128
 KX, M, S, N = 640, 512, 256, 128
 KB = KX // P
 GATE_I, GATE_F, GATE_U, GATE_O = 0, 1, 2, 3
-
+CELL = 3 * P
 WARM_UP = 4
 
 FLOPS = 2 * (KX + P) * M * N
@@ -21,29 +21,33 @@ def tile_deepmultipledecoder_kernel(tc, base, x, h_prev, c_prev, wx, wh, b, offs
         tc.tile_pool(name="held", bufs=1) as held,
         tc.psum_pool(name="psum", bufs=1) as psum,
     ):
-        offsets = held.tile([P, N // 16], U16, name="offsets")
-        nc.sync.dma_start(offsets[:], offs)
-
         b_sb = held.tile([P, 4], F32, name="b_sb")
         with nc.allow_non_contiguous_dma(reason="512 bias values, one to a partition and gate"):
             nc.sync.dma_start(b_sb[:], b.rearrange("(g p) o -> p (g o)", p=P))
 
         h_sb = held.tile([P, N], BF16, name="h_sb")
         nc.scalar.dma_start(h_sb[:], h_prev)
-        wh_sb = held.tile([P, M], BF16, name="wh_sb")
-        nc.scalar.dma_start(wh_sb[:], wh)
         x_sb = held.tile([P, KB, N], BF16, name="x_sb")
         nc.sync.dma_start(x_sb[:], x.rearrange("(p kb) n -> p kb n", kb=KB))
-        wx_blocks = wx.rearrange("(p kb) m -> kb p m", kb=KB)
-        wx_sb = [held.tile([P, M], BF16, name=f"wx_sb{kb}") for kb in range(KB)]
-        for kb in range(KB):
-            queue = nc.sync if kb % 2 == 0 else nc.scalar
-            queue.dma_start(wx_sb[kb][:], wx_blocks[kb])
+        wx_blocks = wx.rearrange("(p kb) m -> p kb m", kb=KB)
 
+        wh_sb = held.tile([P, M], BF16, name="wh_sb")
+        nc.scalar.dma_start(wh_sb[:], wh)
+        wx_cell = []
+        for turn, first in enumerate(range(0, KB, 2)):
+            count = min(2, KB - first)
+            pair = held.tile([P, count, CELL], BF16, name=f"wx_cell{first}")
+            queue = nc.sync if turn % 2 == 0 else nc.scalar
+            queue.dma_start(pair[:], wx_blocks[:, first : first + count, 0:CELL])
+            wx_cell += [pair[:, i, :] for i in range(count)]
         c_sb = held.tile([P, N], F32, name="c_sb")
         nc.sync.dma_start(c_sb[:], c_prev)
+        wx_out = held.tile([P, KB, P], BF16, name="wx_out")
+        nc.scalar.dma_start(wx_out[:], wx_blocks[:, :, CELL:M])
         window = held.tile([P, S], F32, name="window")
         nc.sync.dma_start(window[:], base)
+        offsets = held.tile([P, N // 16], U16, name="offsets")
+        nc.sync.dma_start(offsets[:], offs)
 
         zeros = held.tile([P, 512], BF16, name="zeros")
         nc.vector.memset(zeros[:], 0.0)
@@ -54,16 +58,17 @@ def tile_deepmultipledecoder_kernel(tc, base, x, h_prev, c_prev, wx, wh, b, offs
             nc.tensor.matmul(idle_bank[:], zeros[:, 0:P], zeros[:], start=True, stop=True)
 
         z = [psum.tile([P, N], F32, name=f"z{g}") for g in range(4)]
-        blocks = [(wh_sb, h_sb[:])] + [(wx_sb[kb], x_sb[:, kb, :]) for kb in range(KB)]
-        for k, (weights, moving) in enumerate(blocks):
-            for g in (GATE_F, GATE_I, GATE_U, GATE_O):
+        moving = [h_sb[:]] + [x_sb[:, kb, :] for kb in range(KB)]
+        cell_weights = [wh_sb[:, 0:CELL]] + wx_cell
+        out_weights = [wh_sb[:, CELL:M]] + [wx_out[:, kb, :] for kb in range(KB)]
+        last = len(moving) - 1
+        for k in range(len(moving)):
+            for g in (GATE_F, GATE_I, GATE_U):
                 nc.tensor.matmul(
-                    z[g][:],
-                    weights[:, g * P : (g + 1) * P],
-                    moving,
-                    start=(k == 0),
-                    stop=(k == len(blocks) - 1),
+                    z[g][:], cell_weights[k][:, g * P : (g + 1) * P], moving[k], start=(k == 0), stop=(k == last)
                 )
+        for k in range(len(moving)):
+            nc.tensor.matmul(z[GATE_O][:], out_weights[k], moving[k], start=(k == 0), stop=(k == last))
 
         def gate(g, func, name):
             result = held.tile([P, N], F32, name=name)

@@ -21,9 +21,13 @@ def tile_deepmultipledecoder_kernel(tc, base, x, h_prev, c_prev, wx, wh, b, offs
         tc.tile_pool(name="held", bufs=1) as held,
         tc.psum_pool(name="psum", bufs=1) as psum,
     ):
-        b_sb = held.tile([P, 4], F32, name="b_sb")
-        with nc.allow_non_contiguous_dma(reason="512 bias values, one to a partition and gate"):
-            nc.sync.dma_start(b_sb[:], b.rearrange("(g p) o -> p (g o)", p=P))
+        b_rows = held.tile([P, 32], F32, name="b_rows", align_bytes=64)
+        nc.vector.memset(b_rows[:], 0.0)
+        b_quarters = b.rearrange("(g q r) o -> q g (r o)", g=4, q=4)
+        for q in range(4):
+            nc.sync.dma_start(b_rows[32 * q : 32 * q + 4, :], b_quarters[q])
+        b_sb = held.tile([P, 32], F32, name="b_sb", align_bytes=64)
+        nc.vector.transpose(b_sb[:], b_rows[:])
 
         h_sb = held.tile([P, N], BF16, name="h_sb")
         nc.scalar.dma_start(h_sb[:], h_prev)

@@ -10,7 +10,7 @@ KX, M, S, N = 640, 512, 256, 128
 KB = KX // P
 GATE_I, GATE_F, GATE_U, GATE_O = 0, 1, 2, 3
 CELL = 3 * P
-WARM_UP = 4
+WARM_UP = 3
 
 FLOPS = 2 * (KX + P) * M * N
 
@@ -21,33 +21,31 @@ def tile_deepmultipledecoder_kernel(tc, base, x, h_prev, c_prev, wx, wh, b, offs
         tc.tile_pool(name="held", bufs=1) as held,
         tc.psum_pool(name="psum", bufs=1) as psum,
     ):
-        b_rows = held.tile([P, 32], F32, name="b_rows", align_bytes=64)
-        nc.vector.memset(b_rows[:], 0.0)
-        b_quarters = b.rearrange("(g q r) o -> q g (r o)", g=4, q=4)
-        for q in range(4):
-            nc.sync.dma_start(b_rows[32 * q : 32 * q + 4, :], b_quarters[q])
-        b_sb = held.tile([P, 32], F32, name="b_sb", align_bytes=64)
-        nc.vector.transpose(b_sb[:], b_rows[:])
-
+        wh_sb = held.tile([P, M], BF16, name="wh_sb")
+        nc.sync.dma_start(wh_sb[:], wh)
         h_sb = held.tile([P, N], BF16, name="h_sb")
         nc.scalar.dma_start(h_sb[:], h_prev)
+
         x_sb = held.tile([P, KB, N], BF16, name="x_sb")
         nc.sync.dma_start(x_sb[:], x.rearrange("(p kb) n -> p kb n", kb=KB))
         wx_blocks = wx.rearrange("(p kb) m -> p kb m", kb=KB)
 
-        wh_sb = held.tile([P, M], BF16, name="wh_sb")
-        nc.scalar.dma_start(wh_sb[:], wh)
         wx_cell = []
         for turn, first in enumerate(range(0, KB, 2)):
             count = min(2, KB - first)
             pair = held.tile([P, count, CELL], BF16, name=f"wx_cell{first}")
-            queue = nc.sync if turn % 2 == 0 else nc.scalar
+            queue = nc.scalar if turn % 2 == 0 else nc.sync
             queue.dma_start(pair[:], wx_blocks[:, first : first + count, 0:CELL])
             wx_cell += [pair[:, i, :] for i in range(count)]
+
+        b_sb = held.tile([P, 4], F32, name="b_sb")
+        with nc.allow_non_contiguous_dma(reason="512 bias values, one to a partition and gate"):
+            nc.scalar.dma_start(b_sb[:], b.rearrange("(g p) o -> p (g o)", p=P))
         c_sb = held.tile([P, N], F32, name="c_sb")
         nc.sync.dma_start(c_sb[:], c_prev)
+
         wx_out = held.tile([P, KB, P], BF16, name="wx_out")
-        nc.scalar.dma_start(wx_out[:], wx_blocks[:, :, CELL:M])
+        nc.sync.dma_start(wx_out[:], wx_blocks[:, :, CELL:M])
         window = held.tile([P, S], F32, name="window")
         nc.sync.dma_start(window[:], base)
         offsets = held.tile([P, N // 16], U16, name="offsets")

@@ -21,31 +21,28 @@ def tile_deepmultipledecoder_kernel(tc, base, x, h_prev, c_prev, wx, wh, b, offs
         tc.tile_pool(name="held", bufs=1) as held,
         tc.psum_pool(name="psum", bufs=1) as psum,
     ):
-        wh_sb = held.tile([P, M], BF16, name="wh_sb")
-        nc.sync.dma_start(wh_sb[:], wh)
         h_sb = held.tile([P, N], BF16, name="h_sb")
-        nc.scalar.dma_start(h_sb[:], h_prev)
-
+        nc.sync.dma_start(h_sb[:], h_prev)
         x_sb = held.tile([P, KB, N], BF16, name="x_sb")
         nc.sync.dma_start(x_sb[:], x.rearrange("(p kb) n -> p kb n", kb=KB))
         wx_blocks = wx.rearrange("(p kb) m -> p kb m", kb=KB)
 
         wx_cell = []
-        for turn, first in enumerate(range(0, KB, 2)):
-            count = min(2, KB - first)
-            pair = held.tile([P, count, CELL], BF16, name=f"wx_cell{first}")
-            queue = nc.scalar if turn % 2 == 0 else nc.sync
-            queue.dma_start(pair[:], wx_blocks[:, first : first + count, 0:CELL])
-            wx_cell += [pair[:, i, :] for i in range(count)]
+        for first, count in ((0, 1), (1, 1), (2, 1), (3, 2)):
+            part = held.tile([P, count, CELL], BF16, name=f"wx_cell{first}")
+            nc.sync.dma_start(part[:], wx_blocks[:, first : first + count, 0:CELL])
+            wx_cell += [part[:, i, :] for i in range(count)]
+        wh_sb = held.tile([P, M], BF16, name="wh_sb")
+        nc.sync.dma_start(wh_sb[:], wh)
 
         b_sb = held.tile([P, 4], F32, name="b_sb")
         with nc.allow_non_contiguous_dma(reason="512 bias values, one to a partition and gate"):
-            nc.scalar.dma_start(b_sb[:], b.rearrange("(g p) o -> p (g o)", p=P))
-        c_sb = held.tile([P, N], F32, name="c_sb")
-        nc.sync.dma_start(c_sb[:], c_prev)
+            nc.sync.dma_start(b_sb[:], b.rearrange("(g p) o -> p (g o)", p=P))
 
         wx_out = held.tile([P, KB, P], BF16, name="wx_out")
         nc.sync.dma_start(wx_out[:], wx_blocks[:, :, CELL:M])
+        c_sb = held.tile([P, N], F32, name="c_sb")
+        nc.sync.dma_start(c_sb[:], c_prev)
         window = held.tile([P, S], F32, name="window")
         nc.sync.dma_start(window[:], base)
         offsets = held.tile([P, N // 16], U16, name="offsets")
@@ -60,9 +57,9 @@ def tile_deepmultipledecoder_kernel(tc, base, x, h_prev, c_prev, wx, wh, b, offs
             nc.tensor.matmul(idle_bank[:], zeros[:, 0:P], zeros[:], start=True, stop=True)
 
         z = [psum.tile([P, N], F32, name=f"z{g}") for g in range(4)]
-        moving = [h_sb[:]] + [x_sb[:, kb, :] for kb in range(KB)]
-        cell_weights = [wh_sb[:, 0:CELL]] + wx_cell
-        out_weights = [wh_sb[:, CELL:M]] + [wx_out[:, kb, :] for kb in range(KB)]
+        moving = [x_sb[:, kb, :] for kb in range(KB)] + [h_sb[:]]
+        cell_weights = wx_cell + [wh_sb[:, 0:CELL]]
+        out_weights = [wx_out[:, kb, :] for kb in range(KB)] + [wh_sb[:, CELL:M]]
         last = len(moving) - 1
         for k in range(len(moving)):
             for g in (GATE_F, GATE_I, GATE_U):

@@ -10,6 +10,7 @@ KX, M, S, N = 640, 512, 256, 128
 KB = KX // P
 GATE_I, GATE_F, GATE_U, GATE_O = 0, 1, 2, 3
 CELL = 3 * P
+BLOCK = 32
 WARM_UP = 3
 
 FLOPS = 2 * (KX + P) * M * N
@@ -21,8 +22,18 @@ def tile_deepmultipledecoder_kernel(tc, base, x, h_prev, c_prev, wx, wh, b, offs
         tc.tile_pool(name="held", bufs=1) as held,
         tc.psum_pool(name="psum", bufs=1) as psum,
     ):
-        h_sb = held.tile([P, N], BF16, name="h_sb")
-        nc.sync.dma_start(h_sb[:], h_prev)
+        zeros = held.tile([P, 512], BF16, name="zeros")
+        nc.vector.memset(zeros[:], 0.0)
+
+        b_rows = held.tile([P, 4 * BLOCK], F32, name="b_rows", align_bytes=64)
+        nc.vector.memset(b_rows[:], 0.0)
+        nc.scalar.dma_start(
+            b_rows[:].rearrange("(q s) (g r) -> q s g r", s=BLOCK, r=BLOCK)[:, 0, :, :],
+            b.rearrange("(g q r) o -> q g (r o)", g=4, r=BLOCK),
+        )
+        b_cols = held.tile([P, 4 * BLOCK], F32, name="b_cols", align_bytes=64)
+        nc.vector.transpose(b_cols[:], b_rows[:])
+
         x_sb = held.tile([P, KB, N], BF16, name="x_sb")
         nc.sync.dma_start(x_sb[:], x.rearrange("(p kb) n -> p kb n", kb=KB))
         wx_blocks = wx.rearrange("(p kb) m -> p kb m", kb=KB)
@@ -32,12 +43,10 @@ def tile_deepmultipledecoder_kernel(tc, base, x, h_prev, c_prev, wx, wh, b, offs
             part = held.tile([P, count, CELL], BF16, name=f"wx_cell{first}")
             nc.sync.dma_start(part[:], wx_blocks[:, first : first + count, 0:CELL])
             wx_cell += [part[:, i, :] for i in range(count)]
+        h_sb = held.tile([P, N], BF16, name="h_sb")
+        nc.sync.dma_start(h_sb[:], h_prev)
         wh_sb = held.tile([P, M], BF16, name="wh_sb")
         nc.sync.dma_start(wh_sb[:], wh)
-
-        b_sb = held.tile([P, 4], F32, name="b_sb")
-        with nc.allow_non_contiguous_dma(reason="512 bias values, one to a partition and gate"):
-            nc.sync.dma_start(b_sb[:], b.rearrange("(g p) o -> p (g o)", p=P))
 
         wx_out = held.tile([P, KB, P], BF16, name="wx_out")
         nc.sync.dma_start(wx_out[:], wx_blocks[:, :, CELL:M])
@@ -48,8 +57,6 @@ def tile_deepmultipledecoder_kernel(tc, base, x, h_prev, c_prev, wx, wh, b, offs
         offsets = held.tile([P, N // 16], U16, name="offsets")
         nc.sync.dma_start(offsets[:], offs)
 
-        zeros = held.tile([P, 512], BF16, name="zeros")
-        nc.vector.memset(zeros[:], 0.0)
         early = held.tile([P, 1], F32, name="early")
         nc.scalar.activation(early[:], zeros[:, 0:1], SIGMOID)
         idle_bank = psum.tile([P, 512], F32, name="idle_bank")
@@ -71,7 +78,7 @@ def tile_deepmultipledecoder_kernel(tc, base, x, h_prev, c_prev, wx, wh, b, offs
 
         def gate(g, func, name):
             result = held.tile([P, N], F32, name=name)
-            nc.scalar.activation(result[:], z[g][:], func, bias=b_sb[:, g : g + 1])
+            nc.scalar.activation(result[:], z[g][:], func, bias=b_cols[:, g * BLOCK : g * BLOCK + 1])
             return result
 
         sig_f = gate(GATE_F, SIGMOID, "sig_f")

@@ -39,19 +39,21 @@ def tile_deepmultipledecoder_kernel(tc, base, x, h_prev, c_prev, wx, wh, b, offs
         wx_blocks = wx.rearrange("(p kb) m -> p kb m", kb=KB)
 
         wx_cell = []
-        for first, count in ((0, 1), (1, 1), (2, 1), (3, 2)):
+        for first, count in ((0, 1), (1, 2), (3, 2)):
             part = held.tile([P, count, CELL], BF16, name=f"wx_cell{first}")
             nc.sync.dma_start(part[:], wx_blocks[:, first : first + count, 0:CELL])
             wx_cell += [part[:, i, :] for i in range(count)]
         h_sb = held.tile([P, N], BF16, name="h_sb")
         nc.sync.dma_start(h_sb[:], h_prev)
-        wh_sb = held.tile([P, M], BF16, name="wh_sb")
-        nc.sync.dma_start(wh_sb[:], wh)
+        wh_cell = held.tile([P, CELL], BF16, name="wh_cell")
+        nc.sync.dma_start(wh_cell[:], wh[:, 0:CELL])
 
-        wx_out = held.tile([P, KB, P], BF16, name="wx_out")
-        nc.sync.dma_start(wx_out[:], wx_blocks[:, :, CELL:M])
         c_sb = held.tile([P, N], F32, name="c_sb")
         nc.sync.dma_start(c_sb[:], c_prev)
+        wx_out = held.tile([P, KB, P], BF16, name="wx_out")
+        nc.sync.dma_start(wx_out[:], wx_blocks[:, :, CELL:M])
+        wh_out = held.tile([P, P], BF16, name="wh_out")
+        nc.sync.dma_start(wh_out[:], wh[:, CELL:M])
         window = held.tile([P, S], F32, name="window")
         nc.sync.dma_start(window[:], base)
         offsets = held.tile([P, N // 16], U16, name="offsets")
@@ -65,8 +67,8 @@ def tile_deepmultipledecoder_kernel(tc, base, x, h_prev, c_prev, wx, wh, b, offs
 
         z = [psum.tile([P, N], F32, name=f"z{g}") for g in range(4)]
         moving = [x_sb[:, kb, :] for kb in range(KB)] + [h_sb[:]]
-        cell_weights = wx_cell + [wh_sb[:, 0:CELL]]
-        out_weights = [wx_out[:, kb, :] for kb in range(KB)] + [wh_sb[:, CELL:M]]
+        cell_weights = wx_cell + [wh_cell[:]]
+        out_weights = [wx_out[:, kb, :] for kb in range(KB)] + [wh_out[:]]
         last = len(moving) - 1
         for k in range(len(moving)):
             for g in (GATE_F, GATE_I, GATE_U):

@@ -78,24 +78,34 @@ def tile_deepmultipledecoder_kernel(tc, base, x, h_prev, c_prev, wx, wh, b, offs
         for k in range(len(moving)):
             nc.tensor.matmul(z[GATE_O][:], out_weights[k], moving[k], start=(k == 0), stop=(k == last))
 
-        def gate(g, func, name):
-            result = held.tile([P, N], F32, name=name)
-            nc.scalar.activation(result[:], z[g][:], func, bias=b_cols[:, g * BLOCK : g * BLOCK + 1])
-            return result
+        def gate(result, g, func, columns):
+            nc.scalar.activation(
+                result[:, columns], z[g][:, columns], func, bias=b_cols[:, g * BLOCK : g * BLOCK + 1]
+            )
 
-        sig_f = gate(GATE_F, SIGMOID, "sig_f")
-        sig_i = gate(GATE_I, SIGMOID, "sig_i")
-        tanh_u = gate(GATE_U, TANH, "tanh_u")
-        sig_o = gate(GATE_O, SIGMOID, "sig_o")
-
+        whole = slice(0, N)
+        halves = (slice(0, N // 2), slice(N // 2, N))
+        sig_f = held.tile([P, N], F32, name="sig_f")
+        sig_i = held.tile([P, N], F32, name="sig_i")
+        tanh_u = held.tile([P, N], F32, name="tanh_u")
+        sig_o = held.tile([P, N], F32, name="sig_o")
         kept = held.tile([P, N], F32, name="kept")
-        nc.vector.tensor_tensor(kept[:], sig_f[:], c_sb[:], MULT)
         fresh = held.tile([P, N], F32, name="fresh")
-        nc.vector.tensor_tensor(fresh[:], sig_i[:], tanh_u[:], MULT)
         c_new = held.tile([P, N], F32, name="c_new")
-        nc.vector.tensor_tensor(c_new[:], kept[:], fresh[:], ADD)
         tanh_c = held.tile([P, N], F32, name="tanh_c")
-        nc.scalar.activation(tanh_c[:], c_new[:], TANH)
+
+        gate(sig_f, GATE_F, SIGMOID, whole)
+        nc.vector.tensor_tensor(kept[:], sig_f[:], c_sb[:], MULT)
+        gate(sig_i, GATE_I, SIGMOID, whole)
+        for h in halves:
+            gate(tanh_u, GATE_U, TANH, h)
+        for h in halves:
+            nc.vector.tensor_tensor(fresh[:, h], sig_i[:, h], tanh_u[:, h], MULT)
+        gate(sig_o, GATE_O, SIGMOID, whole)
+        for h in halves:
+            nc.vector.tensor_tensor(c_new[:, h], kept[:, h], fresh[:, h], ADD)
+        for h in halves:
+            nc.scalar.activation(tanh_c[:, h], c_new[:, h], TANH)
 
         nc.vector.tensor_tensor(window[:].indirect(offsets[:]), sig_o[:], tanh_c[:], MULT)
         nc.sync.dma_start(out, window[:])

@@ -12,6 +12,7 @@ GATE_I, GATE_F, GATE_U, GATE_O = 0, 1, 2, 3
 CELL = 3 * P
 BLOCK = 32
 WARM_UP = 3
+WARM_REPEAT = 4
 
 FLOPS = 2 * (KX + P) * M * N
 
@@ -22,8 +23,8 @@ def tile_deepmultipledecoder_kernel(tc, base, x, h_prev, c_prev, wx, wh, b, offs
         tc.tile_pool(name="held", bufs=1) as held,
         tc.psum_pool(name="psum", bufs=1) as psum,
     ):
-        zeros = held.tile([P, 512], BF16, name="zeros")
-        nc.vector.memset(zeros[:], 0.0)
+        zeros = held.tile([P, N], BF16, name="zeros")
+        nc.gpsimd.memset(zeros[:], 0.0)
 
         b_rows = held.tile([P, 4 * BLOCK], F32, name="b_rows", align_bytes=64)
         nc.vector.memset(b_rows[:], 0.0)
@@ -59,11 +60,12 @@ def tile_deepmultipledecoder_kernel(tc, base, x, h_prev, c_prev, wx, wh, b, offs
         offsets = held.tile([P, N // 16], U16, name="offsets")
         nc.sync.dma_start(offsets[:], offs)
 
-        early = held.tile([P, 1], F32, name="early")
-        nc.scalar.activation(early[:], zeros[:, 0:1], SIGMOID)
-        idle_bank = psum.tile([P, 512], F32, name="idle_bank")
+        idle_bank = psum.tile([P, WARM_REPEAT, N], F32, name="idle_bank")
+        repeated = zeros[:].unsqueeze(1).to_broadcast([P, WARM_REPEAT, N])
         for i in range(WARM_UP):
-            nc.tensor.matmul(idle_bank[:], zeros[:, 0:P], zeros[:], start=True, stop=True)
+            nc.tensor.matmul(idle_bank[:], zeros[:], repeated, start=True, stop=True)
+        early = held.tile([P, 1], F32, name="early")
+        nc.scalar.activation(early[:], idle_bank[:, 0, 0:1], SIGMOID)
 
         z = [psum.tile([P, N], F32, name=f"z{g}") for g in range(4)]
         moving = [x_sb[:, kb, :] for kb in range(KB)] + [h_sb[:]]

@@ -9,9 +9,10 @@ P = 128
 KX, M, S, N = 640, 512, 256, 128
 KB = KX // P
 GATE_I, GATE_F, GATE_U, GATE_O = 0, 1, 2, 3
+EARLY = 3
 CELL = 3 * P
 BLOCK = 32
-WARM_UP = 3
+WARM_UP = 4
 WARM_REPEAT = 4
 
 FLOPS = 2 * (KX + P) * M * N
@@ -39,15 +40,16 @@ def tile_deepmultipledecoder_kernel(tc, base, x, h_prev, c_prev, wx, wh, b, offs
         nc.sync.dma_start(x_sb[:], x.rearrange("(p kb) n -> p kb n", kb=KB))
         wx_blocks = wx.rearrange("(p kb) m -> p kb m", kb=KB)
 
-        wx_cell = []
-        for first, count in ((0, 1), (1, 2), (3, 2)):
-            part = held.tile([P, count, CELL], BF16, name=f"wx_cell{first}")
-            nc.sync.dma_start(part[:], wx_blocks[:, first : first + count, 0:CELL])
-            wx_cell += [part[:, i, :] for i in range(count)]
+        wx_early = held.tile([P, EARLY, CELL], BF16, name="wx_early")
+        nc.sync.dma_start(wx_early[:], wx_blocks[:, 0:EARLY, 0:CELL])
+        wx_if = held.tile([P, KB - EARLY, 2 * P], BF16, name="wx_if")
+        nc.sync.dma_start(wx_if[:], wx_blocks[:, EARLY:KB, 0 : 2 * P])
         h_sb = held.tile([P, N], BF16, name="h_sb")
         nc.sync.dma_start(h_sb[:], h_prev)
         wh_cell = held.tile([P, CELL], BF16, name="wh_cell")
         nc.sync.dma_start(wh_cell[:], wh[:, 0:CELL])
+        wx_u = held.tile([P, KB - EARLY, P], BF16, name="wx_u")
+        nc.sync.dma_start(wx_u[:], wx_blocks[:, EARLY:KB, 2 * P : CELL])
 
         c_sb = held.tile([P, N], F32, name="c_sb")
         nc.sync.dma_start(c_sb[:], c_prev)
@@ -68,22 +70,29 @@ def tile_deepmultipledecoder_kernel(tc, base, x, h_prev, c_prev, wx, wh, b, offs
         nc.scalar.activation(early[:], idle_bank[:, 0, 0:1], SIGMOID)
 
         z = [psum.tile([P, N], F32, name=f"z{g}") for g in range(4)]
-        moving = [x_sb[:, kb, :] for kb in range(KB)] + [h_sb[:]]
-        cell_weights = wx_cell + [wh_cell[:]]
-        out_weights = [wx_out[:, kb, :] for kb in range(KB)] + [wh_out[:]]
-        last = len(moving) - 1
-        for k in range(len(moving)):
-            for g in (GATE_F, GATE_I, GATE_U):
-                nc.tensor.matmul(
-                    z[g][:], cell_weights[k][:, g * P : (g + 1) * P], moving[k], start=(k == 0), stop=(k == last)
-                )
-        for k in range(len(moving)):
-            nc.tensor.matmul(z[GATE_O][:], out_weights[k], moving[k], start=(k == 0), stop=(k == last))
 
-        def gate(result, g, func, columns):
-            nc.scalar.activation(
-                result[:, columns], z[g][:, columns], func, bias=b_cols[:, g * BLOCK : g * BLOCK + 1]
-            )
+        def product(g, weights, moving, first=False, last=False):
+            nc.tensor.matmul(z[g][:], weights, moving, start=first, stop=last)
+
+        def columns(g):
+            return slice(g * P, (g + 1) * P)
+
+        for kb in range(EARLY):
+            for g in (GATE_F, GATE_I, GATE_U):
+                product(g, wx_early[:, kb, columns(g)], x_sb[:, kb, :], first=(kb == 0))
+        for kb in range(EARLY, KB):
+            for g in (GATE_F, GATE_I):
+                product(g, wx_if[:, kb - EARLY, columns(g)], x_sb[:, kb, :])
+        for g in (GATE_F, GATE_I, GATE_U):
+            product(g, wh_cell[:, columns(g)], h_sb[:], last=(g != GATE_U))
+        for kb in range(EARLY, KB):
+            product(GATE_U, wx_u[:, kb - EARLY, :], x_sb[:, kb, :], last=(kb == KB - 1))
+        for kb in range(KB):
+            product(GATE_O, wx_out[:, kb, :], x_sb[:, kb, :], first=(kb == 0))
+        product(GATE_O, wh_out[:], h_sb[:], last=True)
+
+        def gate(result, g, func, part):
+            nc.scalar.activation(result[:, part], z[g][:, part], func, bias=b_cols[:, g * BLOCK : g * BLOCK + 1])
 
         whole = slice(0, N)
         halves = (slice(0, N // 2), slice(N // 2, N))

import concourse.mybir as mybir

BF16, F32, U16 = mybir.dt.bfloat16, mybir.dt.float32, mybir.dt.uint16
SIGMOID = mybir.ActivationFunctionType.Sigmoid
TANH = mybir.ActivationFunctionType.Tanh
MULT, ADD = mybir.AluOpType.mult, mybir.AluOpType.add

P = 128
KX, M, S, N = 640, 512, 256, 128
KB = KX // P
GATE_I, GATE_F, GATE_U, GATE_O = 0, 1, 2, 3
EARLY = 3
CELL = 3 * P
BLOCK = 32
WARM_UP = 4
WARM_REPEAT = 4

FLOPS = 2 * (KX + P) * M * N


def tile_deepmultipledecoder_kernel(tc, base, x, h_prev, c_prev, wx, wh, b, offs, out):
    nc = tc.nc
    with (
        tc.tile_pool(name="held", bufs=1) as held,
        tc.psum_pool(name="psum", bufs=1) as psum,
    ):
        zeros = held.tile([P, N], BF16, name="zeros")
        nc.gpsimd.memset(zeros[:], 0.0)

        b_rows = held.tile([P, 4 * BLOCK], F32, name="b_rows", align_bytes=64)
        nc.vector.memset(b_rows[:], 0.0)
        nc.scalar.dma_start(
            b_rows[:].rearrange("(q s) (g r) -> q s g r", s=BLOCK, r=BLOCK)[:, 0, :, :],
            b.rearrange("(g q r) o -> q g (r o)", g=4, r=BLOCK),
        )
        b_cols = held.tile([P, 4 * BLOCK], F32, name="b_cols", align_bytes=64)
        nc.vector.transpose(b_cols[:], b_rows[:])

        x_sb = held.tile([P, KB, N], BF16, name="x_sb")
        nc.sync.dma_start(x_sb[:], x.rearrange("(p kb) n -> p kb n", kb=KB))
        wx_blocks = wx.rearrange("(p kb) m -> p kb m", kb=KB)

        wx_early = held.tile([P, EARLY, CELL], BF16, name="wx_early")
        nc.sync.dma_start(wx_early[:], wx_blocks[:, 0:EARLY, 0:CELL])
        wx_if = held.tile([P, KB - EARLY, 2 * P], BF16, name="wx_if")
        nc.sync.dma_start(wx_if[:], wx_blocks[:, EARLY:KB, 0 : 2 * P])
        h_sb = held.tile([P, N], BF16, name="h_sb")
        nc.sync.dma_start(h_sb[:], h_prev)
        wh_cell = held.tile([P, CELL], BF16, name="wh_cell")
        nc.sync.dma_start(wh_cell[:], wh[:, 0:CELL])
        wx_u = held.tile([P, KB - EARLY, P], BF16, name="wx_u")
        nc.sync.dma_start(wx_u[:], wx_blocks[:, EARLY:KB, 2 * P : CELL])

        c_sb = held.tile([P, N], F32, name="c_sb")
        nc.sync.dma_start(c_sb[:], c_prev)
        wx_out = held.tile([P, KB, P], BF16, name="wx_out")
        nc.sync.dma_start(wx_out[:], wx_blocks[:, :, CELL:M])
        wh_out = held.tile([P, P], BF16, name="wh_out")
        nc.sync.dma_start(wh_out[:], wh[:, CELL:M])
        window = held.tile([P, S], F32, name="window")
        nc.sync.dma_start(window[:], base)
        offsets = held.tile([P, N // 16], U16, name="offsets")
        nc.sync.dma_start(offsets[:], offs)

        idle_bank = psum.tile([P, WARM_REPEAT, N], F32, name="idle_bank")
        repeated = zeros[:].unsqueeze(1).to_broadcast([P, WARM_REPEAT, N])
        for i in range(WARM_UP):
            nc.tensor.matmul(idle_bank[:], zeros[:], repeated, start=True, stop=True)
        early = held.tile([P, 1], F32, name="early")
        nc.scalar.activation(early[:], idle_bank[:, 0, 0:1], SIGMOID)

        z = [psum.tile([P, N], F32, name=f"z{g}") for g in range(4)]

        def product(g, weights, moving, first=False, last=False):
            nc.tensor.matmul(z[g][:], weights, moving, start=first, stop=last)

        def columns(g):
            return slice(g * P, (g + 1) * P)

        for kb in range(EARLY):
            for g in (GATE_F, GATE_I, GATE_U):
                product(g, wx_early[:, kb, columns(g)], x_sb[:, kb, :], first=(kb == 0))
        for kb in range(EARLY, KB):
            for g in (GATE_F, GATE_I):
                product(g, wx_if[:, kb - EARLY, columns(g)], x_sb[:, kb, :])
        for g in (GATE_F, GATE_I, GATE_U):
            product(g, wh_cell[:, columns(g)], h_sb[:], last=(g != GATE_U))
        for kb in range(EARLY, KB):
            product(GATE_U, wx_u[:, kb - EARLY, :], x_sb[:, kb, :], last=(kb == KB - 1))
        for kb in range(KB):
            product(GATE_O, wx_out[:, kb, :], x_sb[:, kb, :], first=(kb == 0))
        product(GATE_O, wh_out[:], h_sb[:], last=True)

        def gate(result, g, func, part):
            nc.scalar.activation(result[:, part], z[g][:, part], func, bias=b_cols[:, g * BLOCK : g * BLOCK + 1])

        whole = slice(0, N)
        halves = (slice(0, N // 2), slice(N // 2, N))
        sig_f = held.tile([P, N], F32, name="sig_f")
        sig_i = held.tile([P, N], F32, name="sig_i")
        tanh_u = held.tile([P, N], F32, name="tanh_u")
        sig_o = held.tile([P, N], F32, name="sig_o")
        kept = held.tile([P, N], F32, name="kept")
        fresh = held.tile([P, N], F32, name="fresh")
        c_new = held.tile([P, N], F32, name="c_new")
        tanh_c = held.tile([P, N], F32, name="tanh_c")

        gate(sig_f, GATE_F, SIGMOID, whole)
        nc.vector.tensor_tensor(kept[:], sig_f[:], c_sb[:], MULT)
        gate(sig_i, GATE_I, SIGMOID, whole)
        for h in halves:
            gate(tanh_u, GATE_U, TANH, h)
        for h in halves:
            nc.vector.tensor_tensor(fresh[:, h], sig_i[:, h], tanh_u[:, h], MULT)
        gate(sig_o, GATE_O, SIGMOID, whole)
        for h in halves:
            nc.vector.tensor_tensor(c_new[:, h], kept[:, h], fresh[:, h], ADD)
        for h in halves:
            nc.scalar.activation(tanh_c[:, h], c_new[:, h], TANH)

        nc.vector.tensor_tensor(window[:].indirect(offsets[:]), sig_o[:], tanh_c[:], MULT)
        nc.sync.dma_start(out, window[:])
